import numpy as np
import ml_dtypes


def mxq(x, axis, fmt="e4m3"):
    dtype, down = {"e4m3": (ml_dtypes.float8_e4m3fn, 7), "e5m2": (ml_dtypes.float8_e5m2, 14)}[fmt]
    v = np.moveaxis(np.asarray(x, np.float32).astype(ml_dtypes.bfloat16).astype(np.float64), axis, -1)
    blocks = v.reshape(v.shape[:-1] + (-1, 32))
    amax = np.abs(blocks).max(-1, keepdims=True)
    byte = np.maximum(np.where(amax > 0, np.frexp(amax)[1] - 1 + 127, 0) - down, 1)
    scale = np.exp2(byte - 127.0)
    codes = (blocks / scale).astype(np.float32).astype(dtype).astype(np.float64)
    return np.moveaxis((codes * scale).reshape(v.shape), -1, axis)


WIDE = False


def mx_kscale(k):
    if not WIDE:
        return np.ones(k)
    levels = np.array([10, -10, 5, -5, 0])
    if k % 512:
        return np.exp2(np.random.permutation(np.resize(levels, k // 32))).repeat(32)
    a = np.empty((k // 512, 16))
    for p in range(k // 512):
        a[p, :8] = np.random.permutation(np.resize(levels, 8))
        for g in range(8):
            far = levels[np.abs(levels - a[p, g]) >= 10]
            a[p, g + 8] = far[np.random.randint(len(far))]
    return np.exp2(a.ravel()).repeat(32)


BF16 = ml_dtypes.bfloat16


def bf(x):
    return np.asarray(x, np.float32).astype(BF16)


def f64(x):
    return np.asarray(x).astype(np.float64)


B, DIN, H1, H2, N, I, K, O = 256, 2048, 16384, 512, 32, 16, 256, 16
NI = N * I
LN_EPS = 1e-5


def setup_inputs():
    s, t = mx_kscale(H1), mx_kscale(H2)
    return {"h1": bf(np.maximum(np.random.standard_normal((B, H1)), 0.0) * s),
            "W2": bf(np.random.standard_normal((H1, H2)) * 1.4 / np.sqrt(H1) / s[:, None] * t),
            "b2": bf(np.random.standard_normal(H2) * 0.2 * t),
            "Wp": bf(np.random.standard_normal((N, H2, I)) * 1.4 / np.sqrt(H2) / t[None, :, None]),
            "bp": bf(np.random.standard_normal((N, I)) * 0.2),
            "ln_g": bf(1.0 + 0.1 * np.random.standard_normal((N, I))),
            "ln_b": bf(0.1 * np.random.standard_normal((N, I)))}


def reference(h1, W2, b2, Wp, bp, ln_g, ln_b):
    x = np.maximum((mxq(f64(h1), 1, "e4m3") @ mxq(f64(W2), 0, "e4m3")) + f64(b2), 0.0)
    wpf = f64(Wp).transpose(1, 0, 2).reshape(H2, NI)
    p = (mxq(x, 1, "e4m3") @ mxq(wpf, 0, "e4m3")).reshape(B, N, I) + f64(bp)
    mu = p.mean(-1, keepdims=True)
    var = ((p - mu) ** 2).mean(-1, keepdims=True)
    return (p - mu) / np.sqrt(var + LN_EPS) * f64(ln_g) + f64(ln_b)

@@ -1,0 +1,353 @@
+from contextlib import ExitStack
+
+import concourse.mybir as mybir
+from concourse.masks import make_identity
+
+F32 = mybir.dt.float32
+BF16 = mybir.dt.bfloat16
+U32 = mybir.dt.uint32
+U8 = mybir.dt.uint8
+FP8X4 = mybir.dt.float8_e4m3fn_x4
+ACT = mybir.ActivationFunctionType
+ALU = mybir.AluOpType
+AXIS = mybir.AxisListType
+
+BATCH, H1, H2, CAPS, CAP_DIM = 256, 16384, 512, 32, 16
+NI = CAPS * CAP_DIM
+LN_EPS = 1e-5
+FLOPS = 2 * BATCH * H1 * H2 + 2 * BATCH * H2 * NI
+
+P = 128
+PACK = 4
+K_PASS = P * PACK
+PASSES = H1 // K_PASS
+ROW_BLOCKS = BATCH // P
+WORD_HALVES = 2
+WORDS = K_PASS // WORD_HALVES
+I_PER_BANK = 8
+
+H1_LOAD_PASSES = 4
+H1_LOADS = PASSES // H1_LOAD_PASSES
+W2_BUFS = 16
+H1_BUFS = W2_BUFS // H1_LOAD_PASSES
+VECTOR_RUNS = 9
+
+RUN = 8
+BLOCKS = H2 // (PACK * RUN)
+
+
+def tile_capsulenetwork_pa_k_kernel(tc, h1, W2, b2, Wp, bp, ln_g, ln_b, out):
+    nc = tc.nc
+    with ExitStack() as ctx:
+        const = ctx.enter_context(tc.tile_pool(name="const", bufs=1))
+        w2_in = ctx.enter_context(tc.tile_pool(name="w2_in", bufs=W2_BUFS))
+        h1_in = ctx.enter_context(tc.tile_pool(name="h1_in", bufs=H1_BUFS))
+        grouped_pool = ctx.enter_context(tc.tile_pool(name="grouped", bufs=3))
+        codes_pool = ctx.enter_context(tc.tile_pool(name="codes", bufs=4))
+        h1_codes_pool = ctx.enter_context(tc.tile_pool(name="h1_codes", bufs=6))
+        norm_pool = ctx.enter_context(tc.tile_pool(name="norm", bufs=ROW_BLOCKS))
+        acc_pool = ctx.enter_context(tc.psum_pool(name="acc", bufs=1))
+        bank_pool = ctx.enter_context(tc.psum_pool(name="bank", bufs=4))
+        ctx.enter_context(tc.manual_schedule())
+
+        w2_raw = {}
+        h1_raw = {}
+        h1_banks = {}
+        w2_grouped, h1_grouped = {}, {}
+        w2_codes, w2_scales, h1_codes, h1_scales = {}, {}, {}, {}
+
+        def load_w2(g):
+            if g >= PASSES:
+                return
+            w2_raw[g] = w2_in.tile([P, PACK * H2], BF16, name="w2_raw")
+            nc.sync.dma_start(
+                out=w2_raw[g][:],
+                in_=W2[g * K_PASS : (g + 1) * K_PASS, :].rearrange("(p j) n -> p (j n)", j=PACK),
+            )
+
+        def load_h1(n):
+            if n >= H1_LOADS:
+                return
+            cols = h1[:, n * H1_LOAD_PASSES * K_PASS : (n + 1) * H1_LOAD_PASSES * K_PASS]
+            h1_raw[n] = h1_in.tile([P, ROW_BLOCKS * H1_LOAD_PASSES * K_PASS], BF16, name="h1_raw")
+            nc.sync.dma_start(
+                out=h1_raw[n][:].rearrange("p (blk k) -> p blk k", blk=ROW_BLOCKS),
+                in_=cols.rearrange("(blk p) k -> p blk k", p=P),
+            )
+
+        ident_f32 = const.tile([P, P], F32)
+        make_identity(nc, ident_f32[:])
+        ident_bf16 = const.tile([P, P], BF16)
+        make_identity(nc, ident_bf16[:])
+        ones = const.tile([P, P], BF16)
+        nc.vector.memset(ones[:], 1.0)
+        eps = const.tile([P, 1], F32)
+        nc.vector.memset(eps[:], LN_EPS)
+
+        vector_rows = const.tile([P, 3 * NI], BF16)
+        nc.vector.memset(vector_rows[:], 0.0)
+        for i, vec in enumerate((bp, ln_g, ln_b)):
+            nc.scalar.dma_start(
+                out=vector_rows[0:1, i * NI : (i + 1) * NI], in_=vec.rearrange("(o n) i -> o (n i)", o=1)
+            )
+        b2_rows = const.tile([P, P], BF16)
+        nc.vector.memset(b2_rows[:], 0.0)
+        nc.scalar.dma_start(
+            out=b2_rows[0:PACK, :].rearrange("t (q r) -> t q r", r=RUN),
+            in_=b2.rearrange("(q t r) -> t q r", t=PACK, r=RUN),
+        )
+
+        sqrt_first = const.tile([P, 1], F32)
+        nc.scalar.activation(out=sqrt_first[:], in_=eps[:], func=ACT.Sqrt)
+
+        spread_banks = []
+        spread = const.tile([P, 3 * NI], BF16)
+        bp_all, g_all, b_all = [spread[:, i * NI : (i + 1) * NI] for i in range(3)]
+        b2_col = const.tile([P, PACK], F32)
+
+        def spread_vectors():
+            for bank in range(2):
+                spread_banks.append(bank_pool.tile([P, 2 * NI], BF16, name="spread_bank", tag="bank"))
+            for i in range(3):
+                nc.tensor.matmul(
+                    out=spread_banks[i // 2][:, (i % 2) * NI : (i % 2 + 1) * NI],
+                    lhsT=ones[:],
+                    rhs=vector_rows[:, i * NI : (i + 1) * NI],
+                    start=True,
+                    stop=True,
+                )
+            nc.tensor.transpose(spread_banks[1][:, NI : NI + P], b2_rows[:], ident_bf16[:])
+
+        def keep_vectors():
+            nc.scalar.copy(out=spread[:, : 2 * NI], in_=spread_banks[0][:])
+            nc.scalar.copy(out=spread[:, 2 * NI :], in_=spread_banks[1][:, :NI])
+            nc.scalar.copy(out=b2_col[:], in_=spread_banks[1][:, NI : NI + PACK])
+
+        wp_raw = const.tile([P, P * CAP_DIM], BF16)
+        for g in range(W2_BUFS):
+            load_w2(g)
+            if g % H1_LOAD_PASSES == 0:
+                load_h1(g // H1_LOAD_PASSES)
+            if g == H1_LOAD_PASSES - 1:
+                wp_by_t = wp_raw[:].rearrange("(n t) (q f) -> t n q f", t=PACK, q=BLOCKS)
+                wp_rows = Wp.rearrange("n (q t r) i -> t n q (r i)", t=PACK, r=RUN)
+                for t in range(PACK):
+                    nc.sync.dma_start(out=wp_by_t[t], in_=wp_rows[t])
+
+        wp_banks = []
+        wp_grouped = const.tile([P, NI * PACK], BF16, align_bytes=64)
+        wp_codes = const.tile([P, NI], U32, align_bytes=64)
+        wp_scales = const.tile([P, NI], U8, align_bytes=64)
+
+        def transpose_wp():
+            wp_by_i = wp_raw[:].rearrange("c (p i) -> c i p", i=CAP_DIM)
+            for first_i in range(0, CAP_DIM, I_PER_BANK):
+                wp_bank = bank_pool.tile([P, I_PER_BANK * P], BF16, tag="bank")
+                for i in range(I_PER_BANK):
+                    nc.tensor.transpose(
+                        wp_bank[:, i * P : (i + 1) * P], wp_by_i[:, first_i + i, :], ident_bf16[:]
+                    )
+                wp_banks.append(wp_bank)
+
+        def regroup_wp():
+            by_cap = wp_grouped[:].rearrange("p (n i t) -> p n i t", i=CAP_DIM, t=PACK)
+            for half, wp_bank in enumerate(wp_banks):
+                nc.scalar.copy(
+                    out=by_cap[:, :, half * I_PER_BANK : (half + 1) * I_PER_BANK, :],
+                    in_=wp_bank[:].rearrange("p (i n t) -> p n i t", i=I_PER_BANK, t=PACK),
+                )
+
+        def quantise_wp():
+            nc.vector.quantize_mx(
+                out=wp_codes[:].bitcast(FP8X4), scales=wp_scales[:], in_=wp_grouped[:]
+            )
+
+        def transpose_h1(g):
+            words = h1_raw[g // H1_LOAD_PASSES][:].bitcast(F32)
+            h1_banks[g] = bank_pool.tile([P, ROW_BLOCKS * WORD_HALVES * P], F32, name="h1_bank", tag="bank")
+            for blk in range(ROW_BLOCKS):
+                first = (blk * H1_LOAD_PASSES + g % H1_LOAD_PASSES) * WORDS
+                for u in range(WORD_HALVES):
+                    plane = (blk * WORD_HALVES + u) * P
+                    nc.tensor.transpose(
+                        h1_banks[g][:, plane : plane + P],
+                        words[:, first + u : first + WORDS : WORD_HALVES],
+                        ident_f32[:],
+                    )
+
+        def regroup_h1(g):
+            h1_grouped[g] = grouped_pool.tile([P, BATCH * PACK], BF16, name="h1_grouped", align_bytes=64)
+            nc.scalar.copy(
+                out=h1_grouped[g][:].bitcast(F32).rearrange(
+                    "p (blk r u) -> p blk r u", blk=ROW_BLOCKS, u=WORD_HALVES
+                ),
+                in_=h1_banks[g][:].rearrange("p (blk u r) -> p blk r u", blk=ROW_BLOCKS, u=WORD_HALVES),
+            )
+
+        def regroup_w2(g):
+            raw = w2_raw[g][:].rearrange("p (j q t r) -> p t q j r", j=PACK, t=PACK, r=RUN)
+            w2_grouped[g] = grouped_pool.tile([P, H2 * PACK], BF16, name="w2_grouped", align_bytes=64)
+            grouped = w2_grouped[g][:].rearrange("p (t q r j) -> p t q j r", t=PACK, r=RUN, j=PACK)
+            nc.vector.tensor_copy(out=grouped[:, :, :VECTOR_RUNS], in_=raw[:, :, :VECTOR_RUNS])
+            nc.scalar.copy(out=grouped[:, :, VECTOR_RUNS:], in_=raw[:, :, VECTOR_RUNS:])
+
+        def quantise_w2(g):
+            w2_codes[g] = codes_pool.tile([P, H2], U32, name="w2_codes", align_bytes=64)
+            w2_scales[g] = codes_pool.tile([P, H2], U8, name="w2_scales", align_bytes=64)
+            nc.vector.quantize_mx(
+                out=w2_codes[g][:].bitcast(FP8X4), scales=w2_scales[g][:], in_=w2_grouped[g][:]
+            )
+
+        def quantise_h1(g):
+            h1_codes[g] = h1_codes_pool.tile([P, BATCH], U32, name="h1_codes", align_bytes=64)
+            h1_scales[g] = h1_codes_pool.tile([P, BATCH], U8, name="h1_scales", align_bytes=64)
+            nc.vector.quantize_mx(
+                out=h1_codes[g][:].bitcast(FP8X4), scales=h1_scales[g][:], in_=h1_grouped[g][:]
+            )
+
+        sums = [acc_pool.tile([P, BATCH], F32, name="sums%d" % t) for t in range(PACK)]
+
+        def multiply(g):
+            for t in range(PACK):
+                cols = slice(t * P, (t + 1) * P)
+                nc.tensor.matmul_mx(
+                    out=sums[t][:],
+                    lhsT=w2_codes[g][:, cols].bitcast(FP8X4),
+                    lhsT_scale=w2_scales[g][:, cols],
+                    rhs=h1_codes[g][:].bitcast(FP8X4),
+                    rhs_scale=h1_scales[g][:],
+                    start=(g == 0),
+                    stop=(g == PASSES - 1),
+                )
+
+        def transpose_pair(g):
+            if g >= PASSES:
+                return
+            transpose_h1(g)
+            transpose_h1(g + 1)
+            if (g + 2) % H1_LOAD_PASSES == 0:
+                load_h1(g // H1_LOAD_PASSES + H1_BUFS)
+
+        def stream_step(s):
+            if s % 2 == 0:
+                transpose_pair(s + 2)
+            if s < PASSES:
+                regroup_w2(s)
+                load_w2(s + W2_BUFS)
+            if s + 1 < PASSES:
+                regroup_h1(s + 1)
+            if 1 <= s <= PASSES:
+                quantise_w2(s - 1)
+            if s < PASSES:
+                quantise_h1(s)
+            if s % 2 == 1 and s >= 3:
+                multiply(s - 3)
+                multiply(s - 2)
+
+        def stream_steps(first, end):
+            for s in range(first, end):
+                stream_step(s)
+
+        transpose_pair(0)
+        regroup_h1(0)
+        stream_steps(0, 2)
+        spread_vectors()
+        stream_steps(2, 4)
+        keep_vectors()
+        transpose_wp()
+        stream_steps(4, 5)
+        regroup_wp()
+        stream_steps(5, 6)
+        quantise_wp()
+        stream_steps(6, PASSES + 2)
+
+        x_planes = const.tile([P, PACK * BATCH], BF16)
+        for t in range(PACK):
+            plane = x_planes[:, t * BATCH : (t + 1) * BATCH]
+            if t % 2 == 0:
+                nc.scalar.activation(out=plane, in_=sums[t][:], func=ACT.Relu, bias=b2_col[:, t : t + 1])
+            else:
+                nc.vector.tensor_scalar(
+                    out=plane, in0=sums[t][:], scalar1=b2_col[:, t : t + 1], scalar2=0.0,
+                    op0=ALU.add, op1=ALU.max,
+                )
+        x_grouped = const.tile([P, BATCH * PACK], BF16, align_bytes=64)
+        nc.vector.tensor_copy(
+            out=x_grouped[:].rearrange("p (b t) -> p b t", t=PACK),
+            in_=x_planes[:].rearrange("p (t b) -> p b t", t=PACK),
+        )
+        x_codes = const.tile([P, BATCH], U32, align_bytes=64)
+        x_scales = const.tile([P, BATCH], U8, align_bytes=64)
+        nc.vector.quantize_mx(out=x_codes[:].bitcast(FP8X4), scales=x_scales[:], in_=x_grouped[:])
+
+        def by_cap(ap):
+            return ap.rearrange("p (n i) -> p n i", i=CAP_DIM)
+
+        def over_cap(ap):
+            return ap.unsqueeze(2).to_broadcast([P, CAPS, CAP_DIM])
+
+        norm = {}
+
+        def norm_tile(name, m, cols):
+            norm[name, m] = norm_pool.tile([P, cols], F32, name=name)
+            return norm[name, m][:]
+
+        blocks = range(ROW_BLOCKS)
+        product = {}
+        for m in blocks:
+            product[m] = bank_pool.tile([P, NI], F32, name="product", tag="bank")
+            rows = slice(m * P, (m + 1) * P)
+            nc.tensor.matmul_mx(
+                out=product[m][:],
+                lhsT=x_codes[:, rows].bitcast(FP8X4),
+                lhsT_scale=x_scales[:, rows],
+                rhs=wp_codes[:].bitcast(FP8X4),
+                rhs_scale=wp_scales[:],
+                start=True,
+                stop=True,
+            )
+        for m in blocks:
+            nc.vector.tensor_tensor(out=norm_tile("u", m, NI), in0=product[m][:], in1=bp_all, op=ALU.add)
+        for m in blocks:
+            nc.vector.tensor_reduce(
+                out=norm_tile("total", m, CAPS), in_=by_cap(norm["u", m][:]), axis=AXIS.X, op=ALU.add
+            )
+        for m in blocks:
+            nc.vector.scalar_tensor_tensor(
+                out=by_cap(norm_tile("dev", m, NI)),
+                in0=over_cap(norm["total", m][:]),
+                scalar=-1.0 / CAP_DIM,
+                in1=by_cap(norm["u", m][:]),
+                op0=ALU.mult,
+                op1=ALU.add,
+            )
+        for m in blocks:
+            nc.scalar.activation(out=norm_tile("dev_sq", m, NI), in_=norm["dev", m][:], func=ACT.Square)
+        for m in blocks:
+            nc.gpsimd.tensor_tensor(
+                out=norm_tile("dev_g", m, NI), in0=norm["dev", m][:], in1=g_all, op=ALU.mult
+            )
+        for m in blocks:
+            nc.vector.tensor_reduce(
+                out=norm_tile("sq_total", m, CAPS), in_=by_cap(norm["dev_sq", m][:]), axis=AXIS.X, op=ALU.add
+            )
+        for m in blocks:
+            nc.scalar.activation(
+                out=norm_tile("std", m, CAPS), in_=norm["sq_total", m][:], func=ACT.Sqrt,
+                scale=1.0 / CAP_DIM, bias=eps[:],
+            )
+        for m in blocks:
+            nc.vector.reciprocal(out=norm_tile("inv_std", m, CAPS), in_=norm["std", m][:])
+        for m in blocks:
+            nc.vector.tensor_tensor(
+                out=by_cap(norm_tile("scaled", m, NI)),
+                in0=by_cap(norm["dev_g", m][:]),
+                in1=over_cap(norm["inv_std", m][:]),
+                op=ALU.mult,
+            )
+        out_rows = out.rearrange("b n i -> b (n i)")
+        for m in blocks:
+            nc.vector.tensor_tensor(
+                out=norm_tile("result", m, NI), in0=norm["scaled", m][:], in1=b_all, op=ALU.add
+            )
+            nc.sync.dma_start(out=out_rows[m * P : (m + 1) * P, :], in_=norm["result", m][:])

@@ -26,14 +26,17 @@ WORD_HALVES = 2
 WORDS = K_PASS // WORD_HALVES
 I_PER_BANK = 8
 
-H1_LOAD_PASSES = 4
-H1_LOADS = PASSES // H1_LOAD_PASSES
+H1_LOAD_SIZES = [2, 2] + [4] * 6 + [2, 2]
+H1_LOAD_FIRST = [sum(H1_LOAD_SIZES[:n]) for n in range(len(H1_LOAD_SIZES))]
+H1_LOAD_MAX = max(H1_LOAD_SIZES)
+H1_BUFS = 6
+H1_LEAD = 2
 W2_BUFS = 16
-H1_BUFS = W2_BUFS // H1_LOAD_PASSES
-VECTOR_RUNS = 9
+VECTOR_RUNS = 8
 
 RUN = 8
 BLOCKS = H2 // (PACK * RUN)
+WP_AFTER = 11
 
 
 def tile_capsulenetwork_pa_k_kernel(tc, h1, W2, b2, Wp, bp, ln_g, ln_b, out):
@@ -65,15 +68,26 @@ def tile_capsulenetwork_pa_k_kernel(tc, h1, W2, b2, Wp, bp, ln_g, ln_b, out):
                 in_=W2[g * K_PASS : (g + 1) * K_PASS, :].rearrange("(p j) n -> p (j n)", j=PACK),
             )
 
-        def load_h1(n):
-            if n >= H1_LOADS:
-                return
-            cols = h1[:, n * H1_LOAD_PASSES * K_PASS : (n + 1) * H1_LOAD_PASSES * K_PASS]
-            h1_raw[n] = h1_in.tile([P, ROW_BLOCKS * H1_LOAD_PASSES * K_PASS], BF16, name="h1_raw")
+        def load_h1(n, blk):
+            if blk == 0:
+                h1_raw[n] = h1_in.tile([P, ROW_BLOCKS * H1_LOAD_MAX * K_PASS], BF16, name="h1_raw")
+            width = H1_LOAD_SIZES[n] * K_PASS
+            at = blk * H1_LOAD_MAX * K_PASS
             nc.sync.dma_start(
-                out=h1_raw[n][:].rearrange("p (blk k) -> p blk k", blk=ROW_BLOCKS),
-                in_=cols.rearrange("(blk p) k -> p blk k", p=P),
+                out=h1_raw[n][:, at : at + width],
+                in_=h1[blk * P : (blk + 1) * P, H1_LOAD_FIRST[n] * K_PASS : H1_LOAD_FIRST[n] * K_PASS + width],
             )
+
+        h1_before = {}
+        for n, first in enumerate(H1_LOAD_FIRST):
+            for blk in range(ROW_BLOCKS):
+                ahead = first - H1_LEAD + blk if H1_LOAD_SIZES[n] == H1_LOAD_MAX else first - 1
+                h1_before.setdefault(max(ahead, 1), []).append((n, blk))
+
+        def load_pass(g):
+            for n, blk in h1_before.get(g, []):
+                load_h1(n, blk)
+            load_w2(g)
 
         ident_f32 = const.tile([P, P], F32)
         make_identity(nc, ident_f32[:])
@@ -125,10 +139,8 @@ def tile_capsulenetwork_pa_k_kernel(tc, h1, W2, b2, Wp, bp, ln_g, ln_b, out):
 
         wp_raw = const.tile([P, P * CAP_DIM], BF16)
         for g in range(W2_BUFS):
-            load_w2(g)
-            if g % H1_LOAD_PASSES == 0:
-                load_h1(g // H1_LOAD_PASSES)
-            if g == H1_LOAD_PASSES - 1:
+            load_pass(g)
+            if g == WP_AFTER:
                 wp_by_t = wp_raw[:].rearrange("(n t) (q f) -> t n q f", t=PACK, q=BLOCKS)
                 wp_rows = Wp.rearrange("n (q t r) i -> t n q (r i)", t=PACK, r=RUN)
                 for t in range(PACK):
@@ -163,10 +175,11 @@ def tile_capsulenetwork_pa_k_kernel(tc, h1, W2, b2, Wp, bp, ln_g, ln_b, out):
             )
 
         def transpose_h1(g):
-            words = h1_raw[g // H1_LOAD_PASSES][:].bitcast(F32)
+            n = max(n for n, first in enumerate(H1_LOAD_FIRST) if first <= g)
+            words = h1_raw[n][:].bitcast(F32)
             h1_banks[g] = bank_pool.tile([P, ROW_BLOCKS * WORD_HALVES * P], F32, name="h1_bank", tag="bank")
             for blk in range(ROW_BLOCKS):
-                first = (blk * H1_LOAD_PASSES + g % H1_LOAD_PASSES) * WORDS
+                first = (blk * H1_LOAD_MAX + g - H1_LOAD_FIRST[n]) * WORDS
                 for u in range(WORD_HALVES):
                     plane = (blk * WORD_HALVES + u) * P
                     nc.tensor.transpose(
@@ -176,9 +189,11 @@ def tile_capsulenetwork_pa_k_kernel(tc, h1, W2, b2, Wp, bp, ln_g, ln_b, out):
                     )
 
         def regroup_h1(g):
-            h1_grouped[g] = grouped_pool.tile([P, BATCH * PACK], BF16, name="h1_grouped", align_bytes=64)
+            if g % 2 == 0:
+                h1_grouped[g // 2] = grouped_pool.tile([P, 2 * BATCH * PACK], BF16, name="h1_grouped", align_bytes=64)
+            half = h1_grouped[g // 2][:, (g % 2) * BATCH * PACK : (g % 2 + 1) * BATCH * PACK]
             nc.scalar.copy(
-                out=h1_grouped[g][:].bitcast(F32).rearrange(
+                out=half.bitcast(F32).rearrange(
                     "p (blk r u) -> p blk r u", blk=ROW_BLOCKS, u=WORD_HALVES
                 ),
                 in_=h1_banks[g][:].rearrange("p (blk u r) -> p blk r u", blk=ROW_BLOCKS, u=WORD_HALVES),
@@ -198,12 +213,15 @@ def tile_capsulenetwork_pa_k_kernel(tc, h1, W2, b2, Wp, bp, ln_g, ln_b, out):
                 out=w2_codes[g][:].bitcast(FP8X4), scales=w2_scales[g][:], in_=w2_grouped[g][:]
             )
 
-        def quantise_h1(g):
-            h1_codes[g] = h1_codes_pool.tile([P, BATCH], U32, name="h1_codes", align_bytes=64)
-            h1_scales[g] = h1_codes_pool.tile([P, BATCH], U8, name="h1_scales", align_bytes=64)
+        def quantise_h1_pair(g):
+            codes = h1_codes_pool.tile([P, 2 * BATCH], U32, name="h1_codes", align_bytes=64)
+            scales = h1_codes_pool.tile([P, 2 * BATCH], U8, name="h1_scales", align_bytes=64)
             nc.vector.quantize_mx(
-                out=h1_codes[g][:].bitcast(FP8X4), scales=h1_scales[g][:], in_=h1_grouped[g][:]
+                out=codes[:].bitcast(FP8X4), scales=scales[:], in_=h1_grouped[g // 2][:]
             )
+            for i in range(2):
+                h1_codes[g + i] = codes[:, i * BATCH : (i + 1) * BATCH]
+                h1_scales[g + i] = scales[:, i * BATCH : (i + 1) * BATCH]
 
         sums = [acc_pool.tile([P, BATCH], F32, name="sums%d" % t) for t in range(PACK)]
 
@@ -214,8 +232,8 @@ def tile_capsulenetwork_pa_k_kernel(tc, h1, W2, b2, Wp, bp, ln_g, ln_b, out):
                     out=sums[t][:],
                     lhsT=w2_codes[g][:, cols].bitcast(FP8X4),
                     lhsT_scale=w2_scales[g][:, cols],
-                    rhs=h1_codes[g][:].bitcast(FP8X4),
-                    rhs_scale=h1_scales[g][:],
+                    rhs=h1_codes[g].bitcast(FP8X4),
+                    rhs_scale=h1_scales[g],
                     start=(g == 0),
                     stop=(g == PASSES - 1),
                 )
@@ -225,24 +243,22 @@ def tile_capsulenetwork_pa_k_kernel(tc, h1, W2, b2, Wp, bp, ln_g, ln_b, out):
                 return
             transpose_h1(g)
             transpose_h1(g + 1)
-            if (g + 2) % H1_LOAD_PASSES == 0:
-                load_h1(g // H1_LOAD_PASSES + H1_BUFS)
 
         def stream_step(s):
             if s % 2 == 0:
                 transpose_pair(s + 2)
             if s < PASSES:
                 regroup_w2(s)
-                load_w2(s + W2_BUFS)
+                load_pass(s + W2_BUFS)
             if s + 1 < PASSES:
                 regroup_h1(s + 1)
             if 1 <= s <= PASSES:
                 quantise_w2(s - 1)
-            if s < PASSES:
-                quantise_h1(s)
-            if s % 2 == 1 and s >= 3:
-                multiply(s - 3)
+            if s % 2 == 1 and s < PASSES:
+                quantise_h1_pair(s - 1)
+            if s % 2 == 0 and s >= 2:
                 multiply(s - 2)
+                multiply(s - 1)
 
         def stream_steps(first, end):
             for s in range(first, end):
@@ -250,16 +266,17 @@ def tile_capsulenetwork_pa_k_kernel(tc, h1, W2, b2, Wp, bp, ln_g, ln_b, out):
 
         transpose_pair(0)
         regroup_h1(0)
-        stream_steps(0, 2)
+        stream_steps(0, 4)
         spread_vectors()
-        stream_steps(2, 4)
+        stream_steps(4, 6)
         keep_vectors()
+        stream_steps(6, 14)
         transpose_wp()
-        stream_steps(4, 5)
+        stream_steps(14, 16)
         regroup_wp()
-        stream_steps(5, 6)
+        stream_steps(16, 18)
         quantise_wp()
-        stream_steps(6, PASSES + 2)
+        stream_steps(18, PASSES + 1)
 
         x_planes = const.tile([P, PACK * BATCH], BF16)
         for t in range(PACK):

@@ -26,17 +26,25 @@ WORD_HALVES = 2
 WORDS = K_PASS // WORD_HALVES
 I_PER_BANK = 8
 
+LEAD = 2
+END_LEAD = 0
+PAIRS = PASSES // 2
 H1_LOAD_SIZES = [2, 2] + [4] * 6 + [2, 2]
 H1_LOAD_FIRST = [sum(H1_LOAD_SIZES[:n]) for n in range(len(H1_LOAD_SIZES))]
 H1_LOAD_MAX = max(H1_LOAD_SIZES)
 H1_BUFS = 6
-H1_LEAD = 2
 W2_BUFS = 16
-VECTOR_RUNS = 8
+WP_TURN = 4
+
+SCALAR_SHARE, SHARES = 7, 16
+SHARED_PASSES = (0, PASSES - 2, PASSES - 1)
 
 RUN = 8
 BLOCKS = H2 // (PACK * RUN)
-WP_AFTER = 11
+
+
+def pair_turn(i):
+    return LEAD + (PASSES - 2 + END_LEAD - LEAD) * i // (PAIRS - 1)
 
 
 def tile_capsulenetwork_pa_k_kernel(tc, h1, W2, b2, Wp, bp, ln_g, ln_b, out):
@@ -45,9 +53,10 @@ def tile_capsulenetwork_pa_k_kernel(tc, h1, W2, b2, Wp, bp, ln_g, ln_b, out):
         const = ctx.enter_context(tc.tile_pool(name="const", bufs=1))
         w2_in = ctx.enter_context(tc.tile_pool(name="w2_in", bufs=W2_BUFS))
         h1_in = ctx.enter_context(tc.tile_pool(name="h1_in", bufs=H1_BUFS))
-        grouped_pool = ctx.enter_context(tc.tile_pool(name="grouped", bufs=3))
-        codes_pool = ctx.enter_context(tc.tile_pool(name="codes", bufs=4))
-        h1_codes_pool = ctx.enter_context(tc.tile_pool(name="h1_codes", bufs=6))
+        grouped_pool = ctx.enter_context(tc.tile_pool(name="grouped", bufs=4))
+        h1_grouped_pool = ctx.enter_context(tc.tile_pool(name="h1_grouped", bufs=3))
+        codes_pool = ctx.enter_context(tc.tile_pool(name="codes", bufs=LEAD + 5))
+        h1_codes_pool = ctx.enter_context(tc.tile_pool(name="h1_codes", bufs=5))
         norm_pool = ctx.enter_context(tc.tile_pool(name="norm", bufs=ROW_BLOCKS))
         acc_pool = ctx.enter_context(tc.psum_pool(name="acc", bufs=1))
         bank_pool = ctx.enter_context(tc.psum_pool(name="bank", bufs=4))
@@ -81,70 +90,91 @@ def tile_capsulenetwork_pa_k_kernel(tc, h1, W2, b2, Wp, bp, ln_g, ln_b, out):
         h1_before = {}
         for n, first in enumerate(H1_LOAD_FIRST):
             for blk in range(ROW_BLOCKS):
-                ahead = first - H1_LEAD + blk if H1_LOAD_SIZES[n] == H1_LOAD_MAX else first - 1
-                h1_before.setdefault(max(ahead, 1), []).append((n, blk))
+                early = 1 - blk if H1_LOAD_SIZES[n] == H1_LOAD_MAX else 0
+                h1_before.setdefault(pair_turn(first // 2) - early, []).append((n, blk))
 
         def load_pass(g):
             for n, blk in h1_before.get(g, []):
                 load_h1(n, blk)
             load_w2(g)
 
+        eps = const.tile([P, 1], F32)
+        nc.vector.memset(eps[:], LN_EPS)
+        first_act = const.tile([P, 1], F32)
+        nc.scalar.activation(out=first_act[:], in_=eps[:], func=ACT.Abs_reciprocal_sqrt)
+
         ident_f32 = const.tile([P, P], F32)
         make_identity(nc, ident_f32[:])
         ident_bf16 = const.tile([P, P], BF16)
         make_identity(nc, ident_bf16[:])
+
+        rows = const.tile([P, P], BF16)
+        nc.vector.memset(rows[:], 0.0)
+        nc.scalar.dma_start(
+            out=rows[0:PACK, :].rearrange("t (q r) -> t q r", r=RUN),
+            in_=b2.rearrange("(q t r) -> t q r", t=PACK, r=RUN),
+        )
+        nc.scalar.dma_start(
+            out=rows[PACK : 2 * PACK, :], in_=bp.rearrange("(c m) i -> c (m i)", c=PACK)
+        )
+        columns = const.tile([P, 2 * PACK], F32)
+
+        def turn_columns():
+            bank = bank_pool.tile([P, P], BF16, name="rows_bank", tag="bank")
+            nc.tensor.transpose(bank[:], rows[:], ident_bf16[:])
+            nc.scalar.copy(out=columns[:], in_=bank[:, : 2 * PACK])
+
         ones = const.tile([P, P], BF16)
         nc.vector.memset(ones[:], 1.0)
-        eps = const.tile([P, 1], F32)
-        nc.vector.memset(eps[:], LN_EPS)
-
-        vector_rows = const.tile([P, 3 * NI], BF16)
+        vector_rows = const.tile([P, 2 * NI], BF16)
         nc.vector.memset(vector_rows[:], 0.0)
-        for i, vec in enumerate((bp, ln_g, ln_b)):
+        for i, vec in enumerate((ln_g, ln_b)):
             nc.scalar.dma_start(
                 out=vector_rows[0:1, i * NI : (i + 1) * NI], in_=vec.rearrange("(o n) i -> o (n i)", o=1)
             )
-        b2_rows = const.tile([P, P], BF16)
-        nc.vector.memset(b2_rows[:], 0.0)
-        nc.scalar.dma_start(
-            out=b2_rows[0:PACK, :].rearrange("t (q r) -> t q r", r=RUN),
-            in_=b2.rearrange("(q t r) -> t q r", t=PACK, r=RUN),
+
+        def spread(i):
+            bank = bank_pool.tile([P, NI], BF16, name="spread_bank", tag="bank")
+            nc.tensor.matmul(
+                out=bank[:], lhsT=ones[:], rhs=vector_rows[:, i * NI : (i + 1) * NI], start=True, stop=True
+            )
+            everywhere = const.tile([P, NI], BF16, name="spread%d" % i)
+            nc.scalar.copy(out=everywhere[:], in_=bank[:])
+            return everywhere
+
+        centre = const.tile([P, P], F32)
+        nc.gpsimd.memset(centre[:], 0.0)
+        by_block = [[-CAP_DIM, P // CAP_DIM], [0, CAP_DIM]]
+        nc.gpsimd.affine_select(
+            out=centre[:], in_=centre[:], compare_op=ALU.is_gt, fill=1.0, base=1 - CAP_DIM,
+            pattern=by_block, channel_multiplier=1,
         )
+        nc.gpsimd.affine_select(
+            out=centre[:], in_=centre[:], compare_op=ALU.is_ge, fill=0.0, base=0,
+            pattern=by_block, channel_multiplier=1,
+        )
+        nc.vector.scalar_tensor_tensor(
+            out=centre[:], in0=centre[:], scalar=-1.0 / CAP_DIM, in1=ident_f32[:], op0=ALU.mult, op1=ALU.add
+        )
+        centre_g = const.tile([P, NI], F32)
 
-        sqrt_first = const.tile([P, 1], F32)
-        nc.scalar.activation(out=sqrt_first[:], in_=eps[:], func=ACT.Sqrt)
-
-        spread_banks = []
-        spread = const.tile([P, 3 * NI], BF16)
-        bp_all, g_all, b_all = [spread[:, i * NI : (i + 1) * NI] for i in range(3)]
-        b2_col = const.tile([P, PACK], F32)
-
-        def spread_vectors():
-            for bank in range(2):
-                spread_banks.append(bank_pool.tile([P, 2 * NI], BF16, name="spread_bank", tag="bank"))
-            for i in range(3):
-                nc.tensor.matmul(
-                    out=spread_banks[i // 2][:, (i % 2) * NI : (i % 2 + 1) * NI],
-                    lhsT=ones[:],
-                    rhs=vector_rows[:, i * NI : (i + 1) * NI],
-                    start=True,
-                    stop=True,
-                )
-            nc.tensor.transpose(spread_banks[1][:, NI : NI + P], b2_rows[:], ident_bf16[:])
-
-        def keep_vectors():
-            nc.scalar.copy(out=spread[:, : 2 * NI], in_=spread_banks[0][:])
-            nc.scalar.copy(out=spread[:, 2 * NI :], in_=spread_banks[1][:, :NI])
-            nc.scalar.copy(out=b2_col[:], in_=spread_banks[1][:, NI : NI + PACK])
+        def make_centre_g():
+            g_all = spread(0)
+            nc.gpsimd.tensor_tensor(
+                out=centre_g[:].rearrange("p (c m) -> p c m", m=P),
+                in0=g_all[:].rearrange("p (c m) -> p c m", m=P),
+                in1=centre[:].unsqueeze(1).to_broadcast([P, NI // P, P]),
+                op=ALU.mult,
+            )
 
         wp_raw = const.tile([P, P * CAP_DIM], BF16)
         for g in range(W2_BUFS):
-            load_pass(g)
-            if g == WP_AFTER:
+            if g == WP_TURN:
                 wp_by_t = wp_raw[:].rearrange("(n t) (q f) -> t n q f", t=PACK, q=BLOCKS)
                 wp_rows = Wp.rearrange("n (q t r) i -> t n q (r i)", t=PACK, r=RUN)
                 for t in range(PACK):
                     nc.sync.dma_start(out=wp_by_t[t], in_=wp_rows[t])
+            load_pass(g)
 
         wp_banks = []
         wp_grouped = const.tile([P, NI * PACK], BF16, align_bytes=64)
@@ -190,7 +220,7 @@ def tile_capsulenetwork_pa_k_kernel(tc, h1, W2, b2, Wp, bp, ln_g, ln_b, out):
 
         def regroup_h1(g):
             if g % 2 == 0:
-                h1_grouped[g // 2] = grouped_pool.tile([P, 2 * BATCH * PACK], BF16, name="h1_grouped", align_bytes=64)
+                h1_grouped[g // 2] = h1_grouped_pool.tile([P, 2 * BATCH * PACK], BF16, name="h1_grouped", align_bytes=64)
             half = h1_grouped[g // 2][:, (g % 2) * BATCH * PACK : (g % 2 + 1) * BATCH * PACK]
             nc.scalar.copy(
                 out=half.bitcast(F32).rearrange(
@@ -203,8 +233,14 @@ def tile_capsulenetwork_pa_k_kernel(tc, h1, W2, b2, Wp, bp, ln_g, ln_b, out):
             raw = w2_raw[g][:].rearrange("p (j q t r) -> p t q j r", j=PACK, t=PACK, r=RUN)
             w2_grouped[g] = grouped_pool.tile([P, H2 * PACK], BF16, name="w2_grouped", align_bytes=64)
             grouped = w2_grouped[g][:].rearrange("p (t q r j) -> p t q j r", t=PACK, r=RUN, j=PACK)
-            nc.vector.tensor_copy(out=grouped[:, :, :VECTOR_RUNS], in_=raw[:, :, :VECTOR_RUNS])
-            nc.scalar.copy(out=grouped[:, :, VECTOR_RUNS:], in_=raw[:, :, VECTOR_RUNS:])
+            if g in SHARED_PASSES:
+                cut = BLOCKS - BLOCKS * SCALAR_SHARE // SHARES
+            else:
+                cut = 0 if SCALAR_SHARE * g % SHARES < SCALAR_SHARE else BLOCKS
+            if cut > 0:
+                nc.vector.tensor_copy(out=grouped[:, :, :cut], in_=raw[:, :, :cut])
+            if cut < BLOCKS:
+                nc.scalar.copy(out=grouped[:, :, cut:], in_=raw[:, :, cut:])
 
         def quantise_w2(g):
             w2_codes[g] = codes_pool.tile([P, H2], U32, name="w2_codes", align_bytes=64)
@@ -223,13 +259,13 @@ def tile_capsulenetwork_pa_k_kernel(tc, h1, W2, b2, Wp, bp, ln_g, ln_b, out):
                 h1_codes[g + i] = codes[:, i * BATCH : (i + 1) * BATCH]
                 h1_scales[g + i] = scales[:, i * BATCH : (i + 1) * BATCH]
 
-        sums = [acc_pool.tile([P, BATCH], F32, name="sums%d" % t) for t in range(PACK)]
+        sums = [acc_pool.tile([P, NI], F32, name="sums%d" % t) for t in range(PACK)]
 
         def multiply(g):
             for t in range(PACK):
                 cols = slice(t * P, (t + 1) * P)
                 nc.tensor.matmul_mx(
-                    out=sums[t][:],
+                    out=sums[t][:, :BATCH],
                     lhsT=w2_codes[g][:, cols].bitcast(FP8X4),
                     lhsT_scale=w2_scales[g][:, cols],
                     rhs=h1_codes[g].bitcast(FP8X4),
@@ -238,54 +274,48 @@ def tile_capsulenetwork_pa_k_kernel(tc, h1, W2, b2, Wp, bp, ln_g, ln_b, out):
                     stop=(g == PASSES - 1),
                 )
 
-        def transpose_pair(g):
-            if g >= PASSES:
-                return
-            transpose_h1(g)
-            transpose_h1(g + 1)
+        pair_at = {pair_turn(i): i for i in range(PAIRS)}
 
         def stream_step(s):
-            if s % 2 == 0:
-                transpose_pair(s + 2)
             if s < PASSES:
                 regroup_w2(s)
                 load_pass(s + W2_BUFS)
-            if s + 1 < PASSES:
-                regroup_h1(s + 1)
-            if 1 <= s <= PASSES:
+            if s in pair_at:
+                for g in (2 * pair_at[s], 2 * pair_at[s] + 1):
+                    transpose_h1(g)
+                for g in (2 * pair_at[s], 2 * pair_at[s] + 1):
+                    regroup_h1(g)
+            if s >= 1 and s <= PASSES:
                 quantise_w2(s - 1)
-            if s % 2 == 1 and s < PASSES:
-                quantise_h1_pair(s - 1)
-            if s % 2 == 0 and s >= 2:
-                multiply(s - 2)
-                multiply(s - 1)
+            if s - 1 in pair_at:
+                quantise_h1_pair(2 * pair_at[s - 1])
+            for g in range(PASSES):
+                if s == max(pair_turn(g // 2) + 2, g + 1):
+                    multiply(g)
 
         def stream_steps(first, end):
             for s in range(first, end):
                 stream_step(s)
 
-        transpose_pair(0)
-        regroup_h1(0)
-        stream_steps(0, 4)
-        spread_vectors()
-        stream_steps(4, 6)
-        keep_vectors()
-        stream_steps(6, 14)
+        stream_steps(0, 1)
+        turn_columns()
+        stream_steps(1, WP_TURN)
+        make_centre_g()
+        stream_steps(WP_TURN, WP_TURN + 1)
         transpose_wp()
-        stream_steps(14, 16)
         regroup_wp()
-        stream_steps(16, 18)
+        stream_steps(WP_TURN + 1, WP_TURN + 2)
         quantise_wp()
-        stream_steps(18, PASSES + 1)
+        stream_steps(WP_TURN + 2, PASSES + 1)
 
         x_planes = const.tile([P, PACK * BATCH], BF16)
         for t in range(PACK):
             plane = x_planes[:, t * BATCH : (t + 1) * BATCH]
             if t % 2 == 0:
-                nc.scalar.activation(out=plane, in_=sums[t][:], func=ACT.Relu, bias=b2_col[:, t : t + 1])
+                nc.scalar.activation(out=plane, in_=sums[t][:, :BATCH], func=ACT.Relu, bias=columns[:, t : t + 1])
             else:
                 nc.vector.tensor_scalar(
-                    out=plane, in0=sums[t][:], scalar1=b2_col[:, t : t + 1], scalar2=0.0,
+                    out=plane, in0=sums[t][:, :BATCH], scalar1=columns[:, t : t + 1], scalar2=0.0,
                     op0=ALU.add, op1=ALU.max,
                 )
         x_grouped = const.tile([P, BATCH * PACK], BF16, align_bytes=64)
@@ -296,12 +326,50 @@ def tile_capsulenetwork_pa_k_kernel(tc, h1, W2, b2, Wp, bp, ln_g, ln_b, out):
         x_codes = const.tile([P, BATCH], U32, align_bytes=64)
         x_scales = const.tile([P, BATCH], U8, align_bytes=64)
         nc.vector.quantize_mx(out=x_codes[:].bitcast(FP8X4), scales=x_scales[:], in_=x_grouped[:])
+        b_all = spread(1)
+
+        u = []
+        for c in range(NI // P):
+            cols = slice(c * P, (c + 1) * P)
+            bank = bank_pool.tile([P, BATCH], F32, name="product", tag="bank")
+            nc.tensor.matmul_mx(
+                out=bank[:],
+                lhsT=wp_codes[:, cols].bitcast(FP8X4),
+                lhsT_scale=wp_scales[:, cols],
+                rhs=x_codes[:].bitcast(FP8X4),
+                rhs_scale=x_scales[:],
+                start=True,
+                stop=True,
+            )
+            u.append(const.tile([P, BATCH], F32, name="u%d" % c))
+            bias = columns[:, PACK + c : PACK + c + 1]
+            if c % 2 == 0:
+                nc.scalar.activation(out=u[c][:], in_=bank[:], func=ACT.Identity, bias=bias)
+            else:
+                nc.vector.tensor_scalar_add(out=u[c][:], in0=bank[:], scalar1=bias)
+
+        blocks = range(ROW_BLOCKS)
+
+        def turn_u(name, tag, m, matrix):
+            bank = acc_pool.tile([P, NI], F32, name=name, tag=tag)
+            for c in range(NI // P):
+                nc.tensor.matmul(
+                    out=bank[:, c * P : (c + 1) * P],
+                    lhsT=u[c][:, m * P : (m + 1) * P],
+                    rhs=matrix(c),
+                    start=True,
+                    stop=True,
+                )
+            return bank
+
+        dev = [turn_u("dev%d" % m, "sums%d" % m, m, lambda c: centre[:]) for m in blocks]
+        dev_g = [
+            turn_u("dev_g%d" % m, "sums%d" % (ROW_BLOCKS + m), m, lambda c: centre_g[:, c * P : (c + 1) * P])
+            for m in blocks
+        ]
 
         def by_cap(ap):
             return ap.rearrange("p (n i) -> p n i", i=CAP_DIM)
-
-        def over_cap(ap):
-            return ap.unsqueeze(2).to_broadcast([P, CAPS, CAP_DIM])
 
         norm = {}
 
@@ -309,62 +377,25 @@ def tile_capsulenetwork_pa_k_kernel(tc, h1, W2, b2, Wp, bp, ln_g, ln_b, out):
             norm[name, m] = norm_pool.tile([P, cols], F32, name=name)
             return norm[name, m][:]
 
-        blocks = range(ROW_BLOCKS)
-        product = {}
         for m in blocks:
-            product[m] = bank_pool.tile([P, NI], F32, name="product", tag="bank")
-            rows = slice(m * P, (m + 1) * P)
-            nc.tensor.matmul_mx(
-                out=product[m][:],
-                lhsT=x_codes[:, rows].bitcast(FP8X4),
-                lhsT_scale=x_scales[:, rows],
-                rhs=wp_codes[:].bitcast(FP8X4),
-                rhs_scale=wp_scales[:],
-                start=True,
-                stop=True,
-            )
-        for m in blocks:
-            nc.vector.tensor_tensor(out=norm_tile("u", m, NI), in0=product[m][:], in1=bp_all, op=ALU.add)
-        for m in blocks:
-            nc.vector.tensor_reduce(
-                out=norm_tile("total", m, CAPS), in_=by_cap(norm["u", m][:]), axis=AXIS.X, op=ALU.add
-            )
-        for m in blocks:
-            nc.vector.scalar_tensor_tensor(
-                out=by_cap(norm_tile("dev", m, NI)),
-                in0=over_cap(norm["total", m][:]),
-                scalar=-1.0 / CAP_DIM,
-                in1=by_cap(norm["u", m][:]),
-                op0=ALU.mult,
-                op1=ALU.add,
-            )
-        for m in blocks:
-            nc.scalar.activation(out=norm_tile("dev_sq", m, NI), in_=norm["dev", m][:], func=ACT.Square)
-        for m in blocks:
-            nc.gpsimd.tensor_tensor(
-                out=norm_tile("dev_g", m, NI), in0=norm["dev", m][:], in1=g_all, op=ALU.mult
-            )
-        for m in blocks:
+            nc.scalar.activation(out=norm_tile("dev_sq", m, NI), in_=dev[m][:], func=ACT.Square)
             nc.vector.tensor_reduce(
                 out=norm_tile("sq_total", m, CAPS), in_=by_cap(norm["dev_sq", m][:]), axis=AXIS.X, op=ALU.add
             )
-        for m in blocks:
             nc.scalar.activation(
-                out=norm_tile("std", m, CAPS), in_=norm["sq_total", m][:], func=ACT.Sqrt,
+                out=norm_tile("inv_std", m, CAPS), in_=norm["sq_total", m][:], func=ACT.Abs_reciprocal_sqrt,
                 scale=1.0 / CAP_DIM, bias=eps[:],
             )
         for m in blocks:
-            nc.vector.reciprocal(out=norm_tile("inv_std", m, CAPS), in_=norm["std", m][:])
-        for m in blocks:
             nc.vector.tensor_tensor(
                 out=by_cap(norm_tile("scaled", m, NI)),
-                in0=by_cap(norm["dev_g", m][:]),
-                in1=over_cap(norm["inv_std", m][:]),
+                in0=by_cap(dev_g[m][:]),
+                in1=norm["inv_std", m][:].unsqueeze(2).to_broadcast([P, CAPS, CAP_DIM]),
                 op=ALU.mult,
             )
         out_rows = out.rearrange("b n i -> b (n i)")
         for m in blocks:
             nc.vector.tensor_tensor(
-                out=norm_tile("result", m, NI), in0=norm["scaled", m][:], in1=b_all, op=ALU.add
+                out=norm_tile("result", m, NI), in0=norm["scaled", m][:], in1=b_all[:], op=ALU.add
             )
             nc.sync.dma_start(out=out_rows[m * P : (m + 1) * P, :], in_=norm["result", m][:])

@@ -290,7 +290,7 @@ def tile_capsulenetwork_pa_k_kernel(tc, h1, W2, b2, Wp, bp, ln_g, ln_b, out):
             if s - 1 in pair_at:
                 quantise_h1_pair(2 * pair_at[s - 1])
             for g in range(PASSES):
-                if s == max(pair_turn(g // 2) + 2, g + 1):
+                if s == min(max(pair_turn(g // 2) + 2 + g % 2, g + 1), PASSES):
                     multiply(g)
 
         def stream_steps(first, end):

@@ -34,6 +34,7 @@ H1_LOAD_FIRST = [sum(H1_LOAD_SIZES[:n]) for n in range(len(H1_LOAD_SIZES))]
 H1_LOAD_MAX = max(H1_LOAD_SIZES)
 H1_BUFS = 6
 W2_BUFS = 16
+IDLE_MATMULS = 3
 WP_TURN = 4
 
 SCALAR_SHARE, SHARES = 7, 16
@@ -159,7 +160,6 @@ def tile_capsulenetwork_pa_k_kernel(tc, h1, W2, b2, Wp, bp, ln_g, ln_b, out):
         centre_g = const.tile([P, NI], F32)
 
         def make_centre_g():
-            g_all = spread(0)
             nc.gpsimd.tensor_tensor(
                 out=centre_g[:].rearrange("p (c m) -> p c m", m=P),
                 in0=g_all[:].rearrange("p (c m) -> p c m", m=P),
@@ -300,6 +300,7 @@ def tile_capsulenetwork_pa_k_kernel(tc, h1, W2, b2, Wp, bp, ln_g, ln_b, out):
         stream_steps(0, 1)
         turn_columns()
         stream_steps(1, WP_TURN)
+        g_all = spread(0)
         make_centre_g()
         stream_steps(WP_TURN, WP_TURN + 1)
         transpose_wp()
@@ -318,55 +319,56 @@ def tile_capsulenetwork_pa_k_kernel(tc, h1, W2, b2, Wp, bp, ln_g, ln_b, out):
                     out=plane, in0=sums[t][:, :BATCH], scalar1=columns[:, t : t + 1], scalar2=0.0,
                     op0=ALU.add, op1=ALU.max,
                 )
-        x_grouped = const.tile([P, BATCH * PACK], BF16, align_bytes=64)
-        nc.vector.tensor_copy(
-            out=x_grouped[:].rearrange("p (b t) -> p b t", t=PACK),
-            in_=x_planes[:].rearrange("p (t b) -> p b t", t=PACK),
-        )
-        x_codes = const.tile([P, BATCH], U32, align_bytes=64)
-        x_scales = const.tile([P, BATCH], U8, align_bytes=64)
-        nc.vector.quantize_mx(out=x_codes[:].bitcast(FP8X4), scales=x_scales[:], in_=x_grouped[:])
         b_all = spread(1)
-
-        u = []
-        for c in range(NI // P):
-            cols = slice(c * P, (c + 1) * P)
-            bank = bank_pool.tile([P, BATCH], F32, name="product", tag="bank")
-            nc.tensor.matmul_mx(
-                out=bank[:],
-                lhsT=wp_codes[:, cols].bitcast(FP8X4),
-                lhsT_scale=wp_scales[:, cols],
-                rhs=x_codes[:].bitcast(FP8X4),
-                rhs_scale=x_scales[:],
-                start=True,
-                stop=True,
-            )
-            u.append(const.tile([P, BATCH], F32, name="u%d" % c))
-            bias = columns[:, PACK + c : PACK + c + 1]
-            if c % 2 == 0:
-                nc.scalar.activation(out=u[c][:], in_=bank[:], func=ACT.Identity, bias=bias)
-            else:
-                nc.vector.tensor_scalar_add(out=u[c][:], in0=bank[:], scalar1=bias)
+        idle_bank = bank_pool.tile([P, NI], BF16, name="idle_bank", tag="bank")
+        for i in range(IDLE_MATMULS):
+            nc.tensor.matmul(out=idle_bank[:], lhsT=ones[:], rhs=vector_rows[:, NI:], start=True, stop=True)
 
         blocks = range(ROW_BLOCKS)
+        x_grouped = [const.tile([P, P * PACK], BF16, name="x_grouped%d" % m, align_bytes=64) for m in blocks]
+        x_codes = [const.tile([P, P], U32, name="x_codes%d" % m, align_bytes=64) for m in blocks]
+        x_scales = [const.tile([P, P], U8, name="x_scales%d" % m, align_bytes=64) for m in blocks]
+        for m in blocks:
+            nc.vector.tensor_copy(
+                out=x_grouped[m][:].rearrange("p (b t) -> p b t", t=PACK),
+                in_=x_planes[:].rearrange("p (t m b) -> p m b t", t=PACK, m=ROW_BLOCKS)[:, m],
+            )
+        for m in blocks:
+            nc.vector.quantize_mx(out=x_codes[m][:].bitcast(FP8X4), scales=x_scales[m][:], in_=x_grouped[m][:])
+
+        u = [const.tile([P, NI], F32, name="u%d" % m) for m in blocks]
+        for m in blocks:
+            for half in range(2):
+                bank = bank_pool.tile([P, 2 * P], F32, name="product", tag="bank")
+                for i in range(2):
+                    c = 2 * half + i
+                    cols = slice(c * P, (c + 1) * P)
+                    nc.tensor.matmul_mx(
+                        out=bank[:, i * P : (i + 1) * P],
+                        lhsT=wp_codes[:, cols].bitcast(FP8X4),
+                        lhsT_scale=wp_scales[:, cols],
+                        rhs=x_codes[m][:].bitcast(FP8X4),
+                        rhs_scale=x_scales[m][:],
+                        start=True,
+                        stop=True,
+                    )
+                for i in range(2):
+                    c = 2 * half + i
+                    bias = columns[:, PACK + c : PACK + c + 1]
+                    part = u[m][:, c * P : (c + 1) * P]
+                    if half == 0:
+                        nc.scalar.activation(out=part, in_=bank[:, i * P : (i + 1) * P], func=ACT.Identity, bias=bias)
+                    else:
+                        nc.vector.tensor_scalar_add(out=part, in0=bank[:, i * P : (i + 1) * P], scalar1=bias)
 
         def turn_u(name, tag, m, matrix):
             bank = acc_pool.tile([P, NI], F32, name=name, tag=tag)
             for c in range(NI // P):
-                nc.tensor.matmul(
-                    out=bank[:, c * P : (c + 1) * P],
-                    lhsT=u[c][:, m * P : (m + 1) * P],
-                    rhs=matrix(c),
-                    start=True,
-                    stop=True,
-                )
+                cols = slice(c * P, (c + 1) * P)
+                nc.tensor.matmul(out=bank[:, cols], lhsT=u[m][:, cols], rhs=matrix(cols), start=True, stop=True)
             return bank
 
-        dev = [turn_u("dev%d" % m, "sums%d" % m, m, lambda c: centre[:]) for m in blocks]
-        dev_g = [
-            turn_u("dev_g%d" % m, "sums%d" % (ROW_BLOCKS + m), m, lambda c: centre_g[:, c * P : (c + 1) * P])
-            for m in blocks
-        ]
+        dev = [turn_u("dev%d" % m, "sums%d" % m, m, lambda cols: centre[:]) for m in blocks]
 
         def by_cap(ap):
             return ap.rearrange("p (n i) -> p n i", i=CAP_DIM)
@@ -377,8 +379,10 @@ def tile_capsulenetwork_pa_k_kernel(tc, h1, W2, b2, Wp, bp, ln_g, ln_b, out):
             norm[name, m] = norm_pool.tile([P, cols], F32, name=name)
             return norm[name, m][:]
 
-        for m in blocks:
+        def square(m):
             nc.scalar.activation(out=norm_tile("dev_sq", m, NI), in_=dev[m][:], func=ACT.Square)
+
+        def inverse_std(m):
             nc.vector.tensor_reduce(
                 out=norm_tile("sq_total", m, CAPS), in_=by_cap(norm["dev_sq", m][:]), axis=AXIS.X, op=ALU.add
             )
@@ -386,16 +390,30 @@ def tile_capsulenetwork_pa_k_kernel(tc, h1, W2, b2, Wp, bp, ln_g, ln_b, out):
                 out=norm_tile("inv_std", m, CAPS), in_=norm["sq_total", m][:], func=ACT.Abs_reciprocal_sqrt,
                 scale=1.0 / CAP_DIM, bias=eps[:],
             )
-        for m in blocks:
+
+        def scale(m, dev_g):
             nc.vector.tensor_tensor(
                 out=by_cap(norm_tile("scaled", m, NI)),
-                in0=by_cap(dev_g[m][:]),
+                in0=by_cap(dev_g[:]),
                 in1=norm["inv_std", m][:].unsqueeze(2).to_broadcast([P, CAPS, CAP_DIM]),
                 op=ALU.mult,
             )
+
         out_rows = out.rearrange("b n i -> b (n i)")
-        for m in blocks:
+
+        def finish(m):
             nc.vector.tensor_tensor(
                 out=norm_tile("result", m, NI), in0=norm["scaled", m][:], in1=b_all[:], op=ALU.add
             )
             nc.sync.dma_start(out=out_rows[m * P : (m + 1) * P, :], in_=norm["result", m][:])
+
+        nc.vector.tensor_tensor(out=norm_tile("dev_g", 0, NI), in0=dev[0][:], in1=g_all[:], op=ALU.mult)
+        square(0)
+        inverse_std(0)
+        dev_g1 = turn_u("dev_g1", "sums%d" % ROW_BLOCKS, 1, lambda cols: centre_g[:, cols])
+        square(1)
+        scale(0, norm["dev_g", 0])
+        inverse_std(1)
+        finish(0)
+        scale(1, dev_g1)
+        finish(1)

@@ -37,8 +37,7 @@ W2_BUFS = 16
 IDLE_MATMULS = 3
 WP_TURN = 4
 
-SCALAR_SHARE, SHARES = 7, 16
-SHARED_PASSES = (0, PASSES - 2, PASSES - 1)
+VECTOR_RUNS = 9
 
 RUN = 8
 BLOCKS = H2 // (PACK * RUN)
@@ -233,14 +232,8 @@ def tile_capsulenetwork_pa_k_kernel(tc, h1, W2, b2, Wp, bp, ln_g, ln_b, out):
             raw = w2_raw[g][:].rearrange("p (j q t r) -> p t q j r", j=PACK, t=PACK, r=RUN)
             w2_grouped[g] = grouped_pool.tile([P, H2 * PACK], BF16, name="w2_grouped", align_bytes=64)
             grouped = w2_grouped[g][:].rearrange("p (t q r j) -> p t q j r", t=PACK, r=RUN, j=PACK)
-            if g in SHARED_PASSES:
-                cut = BLOCKS - BLOCKS * SCALAR_SHARE // SHARES
-            else:
-                cut = 0 if SCALAR_SHARE * g % SHARES < SCALAR_SHARE else BLOCKS
-            if cut > 0:
-                nc.vector.tensor_copy(out=grouped[:, :, :cut], in_=raw[:, :, :cut])
-            if cut < BLOCKS:
-                nc.scalar.copy(out=grouped[:, :, cut:], in_=raw[:, :, cut:])
+            nc.vector.tensor_copy(out=grouped[:, :, :VECTOR_RUNS], in_=raw[:, :, :VECTOR_RUNS])
+            nc.scalar.copy(out=grouped[:, :, VECTOR_RUNS:], in_=raw[:, :, VECTOR_RUNS:])
 
         def quantise_w2(g):
             w2_codes[g] = codes_pool.tile([P, H2], U32, name="w2_codes", align_bytes=64)
@@ -361,14 +354,19 @@ def tile_capsulenetwork_pa_k_kernel(tc, h1, W2, b2, Wp, bp, ln_g, ln_b, out):
                     else:
                         nc.vector.tensor_scalar_add(out=part, in0=bank[:, i * P : (i + 1) * P], scalar1=bias)
 
-        def turn_u(name, tag, m, matrix):
-            bank = acc_pool.tile([P, NI], F32, name=name, tag=tag)
-            for c in range(NI // P):
-                cols = slice(c * P, (c + 1) * P)
-                nc.tensor.matmul(out=bank[:, cols], lhsT=u[m][:, cols], rhs=matrix(cols), start=True, stop=True)
-            return bank
+        def turn_u(bank, m, c, matrix):
+            cols = slice(c * P, (c + 1) * P)
+            nc.tensor.matmul(out=bank, lhsT=u[m][:, cols], rhs=matrix, start=True, stop=True)
 
-        dev = [turn_u("dev%d" % m, "sums%d" % m, m, lambda cols: centre[:]) for m in blocks]
+        dev0 = [acc_pool.tile([P, NI], F32, name="dev0_%d" % half, tag="sums%d" % half) for half in range(2)]
+        dev1 = acc_pool.tile([P, NI], F32, name="dev1", tag="sums2")
+        dev_g1 = acc_pool.tile([P, NI], F32, name="dev_g1", tag="sums3")
+        for c in range(NI // P):
+            turn_u(dev0[c // 2][:, c % 2 * P : (c % 2 + 1) * P], 0, c, centre[:])
+        for c in range(NI // P):
+            turn_u(dev1[:, c * P : (c + 1) * P], 1, c, centre[:])
+        for c in range(NI // P):
+            turn_u(dev_g1[:, c * P : (c + 1) * P], 1, c, centre_g[:, c * P : (c + 1) * P])
 
         def by_cap(ap):
             return ap.rearrange("p (n i) -> p n i", i=CAP_DIM)
@@ -379,8 +377,8 @@ def tile_capsulenetwork_pa_k_kernel(tc, h1, W2, b2, Wp, bp, ln_g, ln_b, out):
             norm[name, m] = norm_pool.tile([P, cols], F32, name=name)
             return norm[name, m][:]
 
-        def square(m):
-            nc.scalar.activation(out=norm_tile("dev_sq", m, NI), in_=dev[m][:], func=ACT.Square)
+        def square(m, dev, cols):
+            nc.scalar.activation(out=norm["dev_sq", m][:, cols], in_=dev, func=ACT.Square)
 
         def inverse_std(m):
             nc.vector.tensor_reduce(
@@ -407,11 +405,18 @@ def tile_capsulenetwork_pa_k_kernel(tc, h1, W2, b2, Wp, bp, ln_g, ln_b, out):
             )
             nc.sync.dma_start(out=out_rows[m * P : (m + 1) * P, :], in_=norm["result", m][:])
 
-        nc.vector.tensor_tensor(out=norm_tile("dev_g", 0, NI), in0=dev[0][:], in1=g_all[:], op=ALU.mult)
-        square(0)
+        for m in blocks:
+            norm_tile("dev_sq", m, NI)
+        norm_tile("dev_g", 0, NI)
+        halves = [slice(half * (NI // 2), (half + 1) * (NI // 2)) for half in range(2)]
+        for half in range(2):
+            square(0, dev0[half][:, : NI // 2], halves[half])
+            other = halves[1 - half]
+            nc.vector.tensor_tensor(
+                out=norm["dev_g", 0][:, other], in0=dev0[1 - half][:, : NI // 2], in1=g_all[:, other], op=ALU.mult
+            )
         inverse_std(0)
-        dev_g1 = turn_u("dev_g1", "sums%d" % ROW_BLOCKS, 1, lambda cols: centre_g[:, cols])
-        square(1)
+        square(1, dev1[:], slice(0, NI))
         scale(0, norm["dev_g", 0])
         inverse_std(1)
         finish(0)

from contextlib import ExitStack

import concourse.mybir as mybir
from concourse.masks import make_identity

F32 = mybir.dt.float32
BF16 = mybir.dt.bfloat16
U32 = mybir.dt.uint32
U8 = mybir.dt.uint8
FP8X4 = mybir.dt.float8_e4m3fn_x4
ACT = mybir.ActivationFunctionType
ALU = mybir.AluOpType
AXIS = mybir.AxisListType

BATCH, H1, H2, CAPS, CAP_DIM = 256, 16384, 512, 32, 16
NI = CAPS * CAP_DIM
LN_EPS = 1e-5
FLOPS = 2 * BATCH * H1 * H2 + 2 * BATCH * H2 * NI

P = 128
PACK = 4
K_PASS = P * PACK
PASSES = H1 // K_PASS
ROW_BLOCKS = BATCH // P
WORD_HALVES = 2
WORDS = K_PASS // WORD_HALVES
I_PER_BANK = 8

LEAD = 2
END_LEAD = 0
PAIRS = PASSES // 2
H1_LOAD_SIZES = [2, 2] + [4] * 6 + [2, 2]
H1_LOAD_FIRST = [sum(H1_LOAD_SIZES[:n]) for n in range(len(H1_LOAD_SIZES))]
H1_LOAD_MAX = max(H1_LOAD_SIZES)
H1_BUFS = 6
W2_BUFS = 16
IDLE_MATMULS = 3
WP_TURN = 4

VECTOR_RUNS = 9

RUN = 8
BLOCKS = H2 // (PACK * RUN)


def pair_turn(i):
    return LEAD + (PASSES - 2 + END_LEAD - LEAD) * i // (PAIRS - 1)


def tile_capsulenetwork_pa_k_kernel(tc, h1, W2, b2, Wp, bp, ln_g, ln_b, out):
    nc = tc.nc
    with ExitStack() as ctx:
        const = ctx.enter_context(tc.tile_pool(name="const", bufs=1))
        w2_in = ctx.enter_context(tc.tile_pool(name="w2_in", bufs=W2_BUFS))
        h1_in = ctx.enter_context(tc.tile_pool(name="h1_in", bufs=H1_BUFS))
        grouped_pool = ctx.enter_context(tc.tile_pool(name="grouped", bufs=4))
        h1_grouped_pool = ctx.enter_context(tc.tile_pool(name="h1_grouped", bufs=3))
        codes_pool = ctx.enter_context(tc.tile_pool(name="codes", bufs=LEAD + 5))
        h1_codes_pool = ctx.enter_context(tc.tile_pool(name="h1_codes", bufs=5))
        norm_pool = ctx.enter_context(tc.tile_pool(name="norm", bufs=ROW_BLOCKS))
        acc_pool = ctx.enter_context(tc.psum_pool(name="acc", bufs=1))
        bank_pool = ctx.enter_context(tc.psum_pool(name="bank", bufs=4))
        ctx.enter_context(tc.manual_schedule())

        w2_raw = {}
        h1_raw = {}
        h1_banks = {}
        w2_grouped, h1_grouped = {}, {}
        w2_codes, w2_scales, h1_codes, h1_scales = {}, {}, {}, {}

        def load_w2(g):
            if g >= PASSES:
                return
            w2_raw[g] = w2_in.tile([P, PACK * H2], BF16, name="w2_raw")
            nc.sync.dma_start(
                out=w2_raw[g][:],
                in_=W2[g * K_PASS : (g + 1) * K_PASS, :].rearrange("(p j) n -> p (j n)", j=PACK),
            )

        def load_h1(n, blk):
            if blk == 0:
                h1_raw[n] = h1_in.tile([P, ROW_BLOCKS * H1_LOAD_MAX * K_PASS], BF16, name="h1_raw")
            width = H1_LOAD_SIZES[n] * K_PASS
            at = blk * H1_LOAD_MAX * K_PASS
            nc.sync.dma_start(
                out=h1_raw[n][:, at : at + width],
                in_=h1[blk * P : (blk + 1) * P, H1_LOAD_FIRST[n] * K_PASS : H1_LOAD_FIRST[n] * K_PASS + width],
            )

        h1_before = {}
        for n, first in enumerate(H1_LOAD_FIRST):
            for blk in range(ROW_BLOCKS):
                early = 1 - blk if H1_LOAD_SIZES[n] == H1_LOAD_MAX else 0
                h1_before.setdefault(pair_turn(first // 2) - early, []).append((n, blk))

        def load_pass(g):
            for n, blk in h1_before.get(g, []):
                load_h1(n, blk)
            load_w2(g)

        eps = const.tile([P, 1], F32)
        nc.vector.memset(eps[:], LN_EPS)
        first_act = const.tile([P, 1], F32)
        nc.scalar.activation(out=first_act[:], in_=eps[:], func=ACT.Abs_reciprocal_sqrt)

        ident_f32 = const.tile([P, P], F32)
        make_identity(nc, ident_f32[:])
        ident_bf16 = const.tile([P, P], BF16)
        make_identity(nc, ident_bf16[:])

        rows = const.tile([P, P], BF16)
        nc.vector.memset(rows[:], 0.0)
        nc.scalar.dma_start(
            out=rows[0:PACK, :].rearrange("t (q r) -> t q r", r=RUN),
            in_=b2.rearrange("(q t r) -> t q r", t=PACK, r=RUN),
        )
        nc.scalar.dma_start(
            out=rows[PACK : 2 * PACK, :], in_=bp.rearrange("(c m) i -> c (m i)", c=PACK)
        )
        columns = const.tile([P, 2 * PACK], F32)

        def turn_columns():
            bank = bank_pool.tile([P, P], BF16, name="rows_bank", tag="bank")
            nc.tensor.transpose(bank[:], rows[:], ident_bf16[:])
            nc.scalar.copy(out=columns[:], in_=bank[:, : 2 * PACK])

        ones = const.tile([P, P], BF16)
        nc.vector.memset(ones[:], 1.0)
        vector_rows = const.tile([P, 2 * NI], BF16)
        nc.vector.memset(vector_rows[:], 0.0)
        for i, vec in enumerate((ln_g, ln_b)):
            nc.scalar.dma_start(
                out=vector_rows[0:1, i * NI : (i + 1) * NI], in_=vec.rearrange("(o n) i -> o (n i)", o=1)
            )

        def spread(i):
            bank = bank_pool.tile([P, NI], BF16, name="spread_bank", tag="bank")
            nc.tensor.matmul(
                out=bank[:], lhsT=ones[:], rhs=vector_rows[:, i * NI : (i + 1) * NI], start=True, stop=True
            )
            everywhere = const.tile([P, NI], BF16, name="spread%d" % i)
            nc.scalar.copy(out=everywhere[:], in_=bank[:])
            return everywhere

        centre = const.tile([P, P], F32)
        nc.gpsimd.memset(centre[:], 0.0)
        by_block = [[-CAP_DIM, P // CAP_DIM], [0, CAP_DIM]]
        nc.gpsimd.affine_select(
            out=centre[:], in_=centre[:], compare_op=ALU.is_gt, fill=1.0, base=1 - CAP_DIM,
            pattern=by_block, channel_multiplier=1,
        )
        nc.gpsimd.affine_select(
            out=centre[:], in_=centre[:], compare_op=ALU.is_ge, fill=0.0, base=0,
            pattern=by_block, channel_multiplier=1,
        )
        nc.vector.scalar_tensor_tensor(
            out=centre[:], in0=centre[:], scalar=-1.0 / CAP_DIM, in1=ident_f32[:], op0=ALU.mult, op1=ALU.add
        )
        centre_g = const.tile([P, NI], F32)

        def make_centre_g():
            nc.gpsimd.tensor_tensor(
                out=centre_g[:].rearrange("p (c m) -> p c m", m=P),
                in0=g_all[:].rearrange("p (c m) -> p c m", m=P),
                in1=centre[:].unsqueeze(1).to_broadcast([P, NI // P, P]),
                op=ALU.mult,
            )

        wp_raw = const.tile([P, P * CAP_DIM], BF16)
        for g in range(W2_BUFS):
            if g == WP_TURN:
                wp_by_t = wp_raw[:].rearrange("(n t) (q f) -> t n q f", t=PACK, q=BLOCKS)
                wp_rows = Wp.rearrange("n (q t r) i -> t n q (r i)", t=PACK, r=RUN)
                for t in range(PACK):
                    nc.sync.dma_start(out=wp_by_t[t], in_=wp_rows[t])
            load_pass(g)

        wp_banks = []
        wp_grouped = const.tile([P, NI * PACK], BF16, align_bytes=64)
        wp_codes = const.tile([P, NI], U32, align_bytes=64)
        wp_scales = const.tile([P, NI], U8, align_bytes=64)

        def transpose_wp():
            wp_by_i = wp_raw[:].rearrange("c (p i) -> c i p", i=CAP_DIM)
            for first_i in range(0, CAP_DIM, I_PER_BANK):
                wp_bank = bank_pool.tile([P, I_PER_BANK * P], BF16, tag="bank")
                for i in range(I_PER_BANK):
                    nc.tensor.transpose(
                        wp_bank[:, i * P : (i + 1) * P], wp_by_i[:, first_i + i, :], ident_bf16[:]
                    )
                wp_banks.append(wp_bank)

        def regroup_wp():
            by_cap = wp_grouped[:].rearrange("p (n i t) -> p n i t", i=CAP_DIM, t=PACK)
            for half, wp_bank in enumerate(wp_banks):
                nc.scalar.copy(
                    out=by_cap[:, :, half * I_PER_BANK : (half + 1) * I_PER_BANK, :],
                    in_=wp_bank[:].rearrange("p (i n t) -> p n i t", i=I_PER_BANK, t=PACK),
                )

        def quantise_wp():
            nc.vector.quantize_mx(
                out=wp_codes[:].bitcast(FP8X4), scales=wp_scales[:], in_=wp_grouped[:]
            )

        def transpose_h1(g):
            n = max(n for n, first in enumerate(H1_LOAD_FIRST) if first <= g)
            words = h1_raw[n][:].bitcast(F32)
            h1_banks[g] = bank_pool.tile([P, ROW_BLOCKS * WORD_HALVES * P], F32, name="h1_bank", tag="bank")
            for blk in range(ROW_BLOCKS):
                first = (blk * H1_LOAD_MAX + g - H1_LOAD_FIRST[n]) * WORDS
                for u in range(WORD_HALVES):
                    plane = (blk * WORD_HALVES + u) * P
                    nc.tensor.transpose(
                        h1_banks[g][:, plane : plane + P],
                        words[:, first + u : first + WORDS : WORD_HALVES],
                        ident_f32[:],
                    )

        def regroup_h1(g):
            if g % 2 == 0:
                h1_grouped[g // 2] = h1_grouped_pool.tile([P, 2 * BATCH * PACK], BF16, name="h1_grouped", align_bytes=64)
            half = h1_grouped[g // 2][:, (g % 2) * BATCH * PACK : (g % 2 + 1) * BATCH * PACK]
            nc.scalar.copy(
                out=half.bitcast(F32).rearrange(
                    "p (blk r u) -> p blk r u", blk=ROW_BLOCKS, u=WORD_HALVES
                ),
                in_=h1_banks[g][:].rearrange("p (blk u r) -> p blk r u", blk=ROW_BLOCKS, u=WORD_HALVES),
            )

        def regroup_w2(g):
            raw = w2_raw[g][:].rearrange("p (j q t r) -> p t q j r", j=PACK, t=PACK, r=RUN)
            w2_grouped[g] = grouped_pool.tile([P, H2 * PACK], BF16, name="w2_grouped", align_bytes=64)
            grouped = w2_grouped[g][:].rearrange("p (t q r j) -> p t q j r", t=PACK, r=RUN, j=PACK)
            nc.vector.tensor_copy(out=grouped[:, :, :VECTOR_RUNS], in_=raw[:, :, :VECTOR_RUNS])
            nc.scalar.copy(out=grouped[:, :, VECTOR_RUNS:], in_=raw[:, :, VECTOR_RUNS:])

        def quantise_w2(g):
            w2_codes[g] = codes_pool.tile([P, H2], U32, name="w2_codes", align_bytes=64)
            w2_scales[g] = codes_pool.tile([P, H2], U8, name="w2_scales", align_bytes=64)
            nc.vector.quantize_mx(
                out=w2_codes[g][:].bitcast(FP8X4), scales=w2_scales[g][:], in_=w2_grouped[g][:]
            )

        def quantise_h1_pair(g):
            codes = h1_codes_pool.tile([P, 2 * BATCH], U32, name="h1_codes", align_bytes=64)
            scales = h1_codes_pool.tile([P, 2 * BATCH], U8, name="h1_scales", align_bytes=64)
            nc.vector.quantize_mx(
                out=codes[:].bitcast(FP8X4), scales=scales[:], in_=h1_grouped[g // 2][:]
            )
            for i in range(2):
                h1_codes[g + i] = codes[:, i * BATCH : (i + 1) * BATCH]
                h1_scales[g + i] = scales[:, i * BATCH : (i + 1) * BATCH]

        sums = [acc_pool.tile([P, NI], F32, name="sums%d" % t) for t in range(PACK)]

        def multiply(g):
            for t in range(PACK):
                cols = slice(t * P, (t + 1) * P)
                nc.tensor.matmul_mx(
                    out=sums[t][:, :BATCH],
                    lhsT=w2_codes[g][:, cols].bitcast(FP8X4),
                    lhsT_scale=w2_scales[g][:, cols],
                    rhs=h1_codes[g].bitcast(FP8X4),
                    rhs_scale=h1_scales[g],
                    start=(g == 0),
                    stop=(g == PASSES - 1),
                )

        pair_at = {pair_turn(i): i for i in range(PAIRS)}

        def stream_step(s):
            if s < PASSES:
                regroup_w2(s)
                load_pass(s + W2_BUFS)
            if s in pair_at:
                for g in (2 * pair_at[s], 2 * pair_at[s] + 1):
                    transpose_h1(g)
                for g in (2 * pair_at[s], 2 * pair_at[s] + 1):
                    regroup_h1(g)
            if s >= 1 and s <= PASSES:
                quantise_w2(s - 1)
            if s - 1 in pair_at:
                quantise_h1_pair(2 * pair_at[s - 1])
            for g in range(PASSES):
                if s == min(max(pair_turn(g // 2) + 2 + g % 2, g + 1), PASSES):
                    multiply(g)

        def stream_steps(first, end):
            for s in range(first, end):
                stream_step(s)

        stream_steps(0, 1)
        turn_columns()
        stream_steps(1, WP_TURN)
        g_all = spread(0)
        make_centre_g()
        stream_steps(WP_TURN, WP_TURN + 1)
        transpose_wp()
        regroup_wp()
        stream_steps(WP_TURN + 1, WP_TURN + 2)
        quantise_wp()
        stream_steps(WP_TURN + 2, PASSES + 1)

        x_planes = const.tile([P, PACK * BATCH], BF16)
        for t in range(PACK):
            plane = x_planes[:, t * BATCH : (t + 1) * BATCH]
            if t % 2 == 0:
                nc.scalar.activation(out=plane, in_=sums[t][:, :BATCH], func=ACT.Relu, bias=columns[:, t : t + 1])
            else:
                nc.vector.tensor_scalar(
                    out=plane, in0=sums[t][:, :BATCH], scalar1=columns[:, t : t + 1], scalar2=0.0,
                    op0=ALU.add, op1=ALU.max,
                )
        b_all = spread(1)
        idle_bank = bank_pool.tile([P, NI], BF16, name="idle_bank", tag="bank")
        for i in range(IDLE_MATMULS):
            nc.tensor.matmul(out=idle_bank[:], lhsT=ones[:], rhs=vector_rows[:, NI:], start=True, stop=True)

        blocks = range(ROW_BLOCKS)
        x_grouped = [const.tile([P, P * PACK], BF16, name="x_grouped%d" % m, align_bytes=64) for m in blocks]
        x_codes = [const.tile([P, P], U32, name="x_codes%d" % m, align_bytes=64) for m in blocks]
        x_scales = [const.tile([P, P], U8, name="x_scales%d" % m, align_bytes=64) for m in blocks]
        for m in blocks:
            nc.vector.tensor_copy(
                out=x_grouped[m][:].rearrange("p (b t) -> p b t", t=PACK),
                in_=x_planes[:].rearrange("p (t m b) -> p m b t", t=PACK, m=ROW_BLOCKS)[:, m],
            )
        for m in blocks:
            nc.vector.quantize_mx(out=x_codes[m][:].bitcast(FP8X4), scales=x_scales[m][:], in_=x_grouped[m][:])

        u = [const.tile([P, NI], F32, name="u%d" % m) for m in blocks]
        for m in blocks:
            for half in range(2):
                bank = bank_pool.tile([P, 2 * P], F32, name="product", tag="bank")
                for i in range(2):
                    c = 2 * half + i
                    cols = slice(c * P, (c + 1) * P)
                    nc.tensor.matmul_mx(
                        out=bank[:, i * P : (i + 1) * P],
                        lhsT=wp_codes[:, cols].bitcast(FP8X4),
                        lhsT_scale=wp_scales[:, cols],
                        rhs=x_codes[m][:].bitcast(FP8X4),
                        rhs_scale=x_scales[m][:],
                        start=True,
                        stop=True,
                    )
                for i in range(2):
                    c = 2 * half + i
                    bias = columns[:, PACK + c : PACK + c + 1]
                    part = u[m][:, c * P : (c + 1) * P]
                    if half == 0:
                        nc.scalar.activation(out=part, in_=bank[:, i * P : (i + 1) * P], func=ACT.Identity, bias=bias)
                    else:
                        nc.vector.tensor_scalar_add(out=part, in0=bank[:, i * P : (i + 1) * P], scalar1=bias)

        def turn_u(bank, m, c, matrix):
            cols = slice(c * P, (c + 1) * P)
            nc.tensor.matmul(out=bank, lhsT=u[m][:, cols], rhs=matrix, start=True, stop=True)

        dev0 = [acc_pool.tile([P, NI], F32, name="dev0_%d" % half, tag="sums%d" % half) for half in range(2)]
        dev1 = acc_pool.tile([P, NI], F32, name="dev1", tag="sums2")
        dev_g1 = acc_pool.tile([P, NI], F32, name="dev_g1", tag="sums3")
        for c in range(NI // P):
            turn_u(dev0[c // 2][:, c % 2 * P : (c % 2 + 1) * P], 0, c, centre[:])
        for c in range(NI // P):
            turn_u(dev1[:, c * P : (c + 1) * P], 1, c, centre[:])
        for c in range(NI // P):
            turn_u(dev_g1[:, c * P : (c + 1) * P], 1, c, centre_g[:, c * P : (c + 1) * P])

        def by_cap(ap):
            return ap.rearrange("p (n i) -> p n i", i=CAP_DIM)

        norm = {}

        def norm_tile(name, m, cols):
            norm[name, m] = norm_pool.tile([P, cols], F32, name=name)
            return norm[name, m][:]

        def square(m, dev, cols):
            nc.scalar.activation(out=norm["dev_sq", m][:, cols], in_=dev, func=ACT.Square)

        def inverse_std(m):
            nc.vector.tensor_reduce(
                out=norm_tile("sq_total", m, CAPS), in_=by_cap(norm["dev_sq", m][:]), axis=AXIS.X, op=ALU.add
            )
            nc.scalar.activation(
                out=norm_tile("inv_std", m, CAPS), in_=norm["sq_total", m][:], func=ACT.Abs_reciprocal_sqrt,
                scale=1.0 / CAP_DIM, bias=eps[:],
            )

        def scale(m, dev_g):
            nc.vector.tensor_tensor(
                out=by_cap(norm_tile("scaled", m, NI)),
                in0=by_cap(dev_g[:]),
                in1=norm["inv_std", m][:].unsqueeze(2).to_broadcast([P, CAPS, CAP_DIM]),
                op=ALU.mult,
            )

        out_rows = out.rearrange("b n i -> b (n i)")

        def finish(m):
            nc.vector.tensor_tensor(
                out=norm_tile("result", m, NI), in0=norm["scaled", m][:], in1=b_all[:], op=ALU.add
            )
            nc.sync.dma_start(out=out_rows[m * P : (m + 1) * P, :], in_=norm["result", m][:])

        for m in blocks:
            norm_tile("dev_sq", m, NI)
        norm_tile("dev_g", 0, NI)
        halves = [slice(half * (NI // 2), (half + 1) * (NI // 2)) for half in range(2)]
        for half in range(2):
            square(0, dev0[half][:, : NI // 2], halves[half])
            other = halves[1 - half]
            nc.vector.tensor_tensor(
                out=norm["dev_g", 0][:, other], in0=dev0[1 - half][:, : NI // 2], in1=g_all[:, other], op=ALU.mult
            )
        inverse_std(0)
        square(1, dev1[:], slice(0, NI))
        scale(0, norm["dev_g", 0])
        inverse_std(1)
        finish(0)
        scale(1, dev_g1)
        finish(1)
